import numpy as np
import ml_dtypes


def mxq(x, axis, fmt="e4m3"):
    dtype, down = {"e4m3": (ml_dtypes.float8_e4m3fn, 7), "e5m2": (ml_dtypes.float8_e5m2, 14)}[fmt]
    v = np.moveaxis(np.asarray(x, np.float32).astype(ml_dtypes.bfloat16).astype(np.float64), axis, -1)
    blocks = v.reshape(v.shape[:-1] + (-1, 32))
    amax = np.abs(blocks).max(-1, keepdims=True)
    byte = np.maximum(np.where(amax > 0, np.frexp(amax)[1] - 1 + 127, 0) - down, 1)
    scale = np.exp2(byte - 127.0)
    codes = (blocks / scale).astype(np.float32).astype(dtype).astype(np.float64)
    return np.moveaxis((codes * scale).reshape(v.shape), -1, axis)


WIDE = False


def mx_kscale(k):
    if not WIDE:
        return np.ones(k)
    levels = np.array([10, -10, 5, -5, 0])
    a = np.random.permutation(np.resize(levels, k // 512 * 4)).reshape(k // 512, 4)
    idx = np.arange(k)
    return np.exp2(a[idx // 512, idx % 128 // 32])


BF16 = ml_dtypes.bfloat16


def bf(x):
    return np.asarray(x, np.float32).astype(BF16)


def f64(x):
    return np.asarray(x).astype(np.float64)


N1, N2, D = 1024, 512, 512

SQRT5 = np.sqrt(5.0)


def setup_inputs():
    s = mx_kscale(D)
    g = np.random.standard_normal((1, D))
    x1 = np.random.standard_normal((N1, 1)) * g + 0.6 * np.random.standard_normal((N1, D))
    x2 = np.random.standard_normal((N2, 1)) * g + 0.6 * np.random.standard_normal((N2, D))
    x2[: N2 // 4] = x1[: N2 // 4]
    x1[-(N1 // 4):] *= (s * s)[None, :]
    x2[-(N2 // 4):] *= (s * s)[None, :]
    return {"X1": bf(x1), "X2": bf(x2),
            "c": bf(np.random.uniform(size=(1,)) + 0.5),
            "l": bf((np.random.uniform(size=(D,)) + 0.5) * 2.0 * np.sqrt(D))}


def reference(X1, X2, c, l):
    X1_l = f64(X1) / f64(l)
    X2_l = f64(X2) / f64(l)
    sq1 = np.sum(X1_l * X1_l, axis=-1)
    sq2 = np.sum(X2_l * X2_l, axis=-1)
    cross = mxq(X1_l, 1, "e4m3") @ mxq(X2_l, 1, "e4m3").T
    d2 = np.maximum(sq1[:, None] + sq2[None, :] - 2.0 * cross, 0.0)
    r = np.sqrt(d2)
    c2 = np.squeeze(f64(c) * f64(c))
    return c2 * (1.0 + SQRT5 * r + (5.0 / 3.0) * (r * r)) * np.exp(-SQRT5 * r)

@@ -1,0 +1,205 @@
+import math
+from contextlib import ExitStack
+
+import concourse.mybir as mybir
+from concourse.masks import make_identity
+
+F32 = mybir.dt.float32
+BF16 = mybir.dt.bfloat16
+U32 = mybir.dt.uint32
+U8 = mybir.dt.uint8
+FP8X4 = mybir.dt.float8_e4m3fn_x4
+ALU = mybir.AluOpType
+ACT = mybir.ActivationFunctionType
+
+P = 128
+PACK = 4
+N1, N2, D = 1024, 512, 512
+assert D == P * PACK
+X1_TILES = N1 // P
+X2_TILES = N2 // P
+POINT_TILES = X2_TILES + X1_TILES
+LOAD_TILES = 2
+
+FLOPS = 2 * N1 * N2 * D
+
+
+def tile_matern52_s_kernel(tc, X1, X2, c, l, out):
+    nc = tc.nc
+    with ExitStack() as stack:
+        keep = stack.enter_context(tc.tile_pool(name="keep", bufs=1))
+        work = stack.enter_context(tc.tile_pool(name="work", bufs=3))
+        psum_rows = stack.enter_context(tc.psum_pool(name="psum_rows", bufs=2))
+        psum_flip = stack.enter_context(tc.psum_pool(name="psum_flip", bufs=3))
+        psum_cross = stack.enter_context(tc.psum_pool(name="psum_cross", bufs=3))
+        stack.enter_context(tc.manual_schedule())
+
+        l_sb = keep.tile([P, PACK], BF16)
+        nc.sync.dma_start(out=l_sb[:], in_=l.rearrange("(p t) -> p t", t=PACK))
+        c_sb = keep.tile([P, 1], BF16)
+        nc.scalar.dma_start(out=c_sb[:], in_=c.partition_broadcast(P))
+        x2_sb = keep.tile([P, X2_TILES, D], BF16)
+        x2_view = X2.rearrange("(j p) d -> p j d", p=P)
+        for j in range(0, X2_TILES, LOAD_TILES):
+            nc.sync.dma_start(out=x2_sb[:, j : j + LOAD_TILES, :], in_=x2_view[:, j : j + LOAD_TILES, :])
+        x1_sb = keep.tile([P, X1_TILES, D], BF16)
+        x1_view = X1.rearrange("(p i) d -> p i d", i=X1_TILES)
+        out_view = out.rearrange("(p i) m -> p i m", i=X1_TILES)
+        for i in range(0, X1_TILES, LOAD_TILES):
+            nc.sync.dma_start(out=x1_sb[:, i : i + LOAD_TILES, :], in_=x1_view[:, i : i + LOAD_TILES, :])
+
+        ident = keep.tile([P, P], F32)
+        make_identity(nc, ident[:])
+        one = keep.tile([P, 1], F32)
+        nc.vector.memset(one[:], 1.0)
+        warm = keep.tile([P, 1], F32)
+        nc.scalar.activation(out=warm[:], in_=one[:], func=ACT.Sqrt)
+
+        def repeat_on_all_partitions(columns, count):
+            rows = psum_rows.tile([P, count, P], F32, name="rows", tag="rows")
+            for j in range(count):
+                nc.tensor.transpose(rows[:, j, :], columns[:, j : j + 1].to_broadcast([P, P]), ident[:])
+            return rows
+
+        inv_l = keep.tile([P, PACK], F32)
+        nc.vector.reciprocal(out=inv_l[:], in_=l_sb[:])
+        inv_l_rows = keep.tile([P, PACK, P], F32)
+        nc.vector.tensor_copy(out=inv_l_rows[:], in_=repeat_on_all_partitions(inv_l, PACK)[:])
+
+        poly_scale = keep.tile([P, 1], F32)
+        poly_bias = keep.tile([P, 1], F32)
+        c_f32 = keep.tile([P, 1], F32)
+        c_quarter = keep.tile([P, 1], F32)
+        poly_add = keep.tile([P, 1], F32)
+        for scalar_tile, factor in (
+            (poly_scale, 1.0 / math.sqrt(3.0)),
+            (poly_bias, 1.5 / math.sqrt(3.0)),
+            (c_f32, 1.0),
+            (c_quarter, 0.25),
+        ):
+            nc.gpsimd.tensor_scalar(
+                out=scalar_tile[:], in0=c_sb[:], scalar1=factor, scalar2=0.0, op0=ALU.mult, op1=ALU.add
+            )
+        nc.gpsimd.tensor_tensor(out=poly_add[:], in0=c_quarter[:], in1=c_f32[:], op=ALU.mult)
+
+        a_codes = keep.tile([P, X1_TILES, P], U32, align_bytes=64)
+        a_scales = keep.tile([P, X1_TILES, P], U8, align_bytes=64)
+        b_codes = keep.tile([P, X2_TILES, P], U32, align_bytes=64)
+        b_scales = keep.tile([P, X2_TILES, P], U8, align_bytes=64)
+        sq1 = keep.tile([P, X1_TILES], F32)
+        sq2 = keep.tile([P, X2_TILES], F32)
+        sq2_rows = keep.tile([P, X2_TILES, P], F32)
+        s_all = keep.tile([P, X1_TILES, N2], F32)
+        w_all = keep.tile([P, X1_TILES, N2], F32)
+
+        def points(j):
+            if j < X2_TILES:
+                return x2_sb[:, j, :], b_codes[:, j, :], b_scales[:, j, :], sq2[:, j : j + 1]
+            i = j - X2_TILES
+            return x1_sb[:, i, :], a_codes[:, i, :], a_scales[:, i, :], sq1[:, i : i + 1]
+
+        scaled, flipped, grouped, cross, part, d2 = {}, {}, {}, {}, {}, {}
+
+        def scale(j):
+            scaled[j] = work.tile([P, PACK, P], F32, name="scaled", tag="scaled")
+            nc.vector.tensor_tensor(
+                out=scaled[j][:],
+                in0=points(j)[0].rearrange("n (p t) -> n t p", t=PACK),
+                in1=inv_l_rows[:],
+                op=ALU.mult,
+            )
+
+        def sum_squares(j):
+            squares = work.tile([P, PACK, P], F32, name="squares", tag="squares")
+            nc.scalar.activation(out=squares[:], in_=scaled[j][:], func=ACT.Square, accum_out=points(j)[3])
+
+        def flip(j):
+            flipped[j] = psum_flip.tile([P, PACK, P], F32, name="flipped", tag="flipped")
+            for t in range(PACK):
+                nc.tensor.transpose(flipped[j][:, t, :], scaled[j][:, t, :], ident[:])
+
+        def regroup(j):
+            grouped[j] = work.tile([P, P, PACK], BF16, name="grouped", tag="grouped", align_bytes=64)
+            planes = flipped[j][:].rearrange("p t n -> p n t")
+            if j % 2 == 0:
+                nc.vector.tensor_copy(out=grouped[j][:], in_=planes)
+            else:
+                nc.scalar.copy(out=grouped[j][:], in_=planes)
+
+        def quantise(j):
+            nc.vector.quantize_mx(
+                out=points(j)[1].bitcast(FP8X4),
+                scales=points(j)[2],
+                in_=grouped[j][:].rearrange("p n t -> p (n t)"),
+            )
+
+        def spread_sq2():
+            nc.scalar.copy(out=sq2_rows[:], in_=repeat_on_all_partitions(sq2, X2_TILES)[:])
+
+        def multiply(i):
+            cross[i] = psum_cross.tile([P, N2], F32, name="cross", tag="cross")
+            nc.tensor.matmul_mx(
+                out=cross[i][:],
+                lhsT=a_codes[:, i, :].bitcast(FP8X4),
+                lhsT_scale=a_scales[:, i, :],
+                rhs=b_codes[:].rearrange("p j n -> p (j n)").bitcast(FP8X4),
+                rhs_scale=b_scales[:].rearrange("p j n -> p (j n)"),
+                start=True,
+                stop=True,
+            )
+
+        def bracket(i):
+            part[i] = work.tile([P, N2], F32, name="part", tag="part")
+            nc.vector.scalar_tensor_tensor(
+                out=part[i][:],
+                in0=cross[i][:],
+                scalar=-2.0,
+                in1=sq2_rows[:].rearrange("p j n -> p (j n)"),
+                op0=ALU.mult,
+                op1=ALU.add,
+            )
+
+        def clamp(i):
+            d2[i] = work.tile([P, N2], F32, name="d2", tag="d2")
+            nc.vector.tensor_scalar(
+                out=d2[i][:], in0=part[i][:], scalar1=sq1[:, i : i + 1], scalar2=0.0, op0=ALU.add, op1=ALU.max
+            )
+
+        def root(i):
+            nc.scalar.activation(out=s_all[:, i, :], in_=d2[i][:], func=ACT.Sqrt, scale=5.0)
+
+        def polynomial(i):
+            nc.scalar.activation(
+                out=w_all[:, i, :], in_=s_all[:, i, :], func=ACT.Square, scale=poly_scale[:], bias=poly_bias[:]
+            )
+
+        def decay_finish_store(i):
+            decay = work.tile([P, N2], F32, name="decay", tag="decay")
+            nc.scalar.activation(out=decay[:], in_=s_all[:, i, :], func=ACT.Exp, scale=-1.0)
+            result = work.tile([P, N2], F32, name="result", tag="result")
+            nc.vector.scalar_tensor_tensor(
+                out=result[:], in0=w_all[:, i, :], scalar=poly_add[:], in1=decay[:], op0=ALU.add, op1=ALU.mult
+            )
+            nc.sync.dma_start(out=out_view[:, i, :], in_=result[:])
+
+        def due(stage, index, count):
+            if 0 <= index < count:
+                stage(index)
+
+        X1_LAG = X2_TILES + 3
+        for k in range(X1_TILES + X1_LAG + 1):
+            due(multiply, k - X1_LAG, X1_TILES)
+            if k == X2_TILES + 1:
+                spread_sq2()
+            due(scale, k, POINT_TILES)
+            due(regroup, k - 1, POINT_TILES)
+            due(flip, k, POINT_TILES)
+            due(bracket, k - X1_LAG, X1_TILES)
+            due(root, k - X1_LAG - 1, X1_TILES)
+            due(quantise, k - 2, POINT_TILES)
+            due(sum_squares, k, POINT_TILES)
+            due(clamp, k - X1_LAG, X1_TILES)
+            due(polynomial, k - X1_LAG - 1, X1_TILES)
+
+        for i in range(X1_TILES):
+            decay_finish_store(i)

@@ -21,6 +21,11 @@ X2_TILES = N2 // P
 POINT_TILES = X2_TILES + X1_TILES
 LOAD_TILES = 2
 
+REGROUP_LAG = 2
+QUANTISE_LAG = 3
+MULTIPLY_LAG = 5
+ROOT_LAG = 6
+
 FLOPS = 2 * N1 * N2 * D
 
 
@@ -29,9 +34,10 @@ def tile_matern52_s_kernel(tc, X1, X2, c, l, out):
     with ExitStack() as stack:
         keep = stack.enter_context(tc.tile_pool(name="keep", bufs=1))
         work = stack.enter_context(tc.tile_pool(name="work", bufs=3))
+        scaled_pool = stack.enter_context(tc.tile_pool(name="scaled_pool", bufs=4))
         psum_rows = stack.enter_context(tc.psum_pool(name="psum_rows", bufs=2))
-        psum_flip = stack.enter_context(tc.psum_pool(name="psum_flip", bufs=3))
-        psum_cross = stack.enter_context(tc.psum_pool(name="psum_cross", bufs=3))
+        psum_flip = stack.enter_context(tc.psum_pool(name="psum_flip", bufs=4))
+        psum_cross = stack.enter_context(tc.psum_pool(name="psum_cross", bufs=2))
         stack.enter_context(tc.manual_schedule())
 
         l_sb = keep.tile([P, PACK], BF16)
@@ -63,8 +69,7 @@ def tile_matern52_s_kernel(tc, X1, X2, c, l, out):
 
         inv_l = keep.tile([P, PACK], F32)
         nc.vector.reciprocal(out=inv_l[:], in_=l_sb[:])
-        inv_l_rows = keep.tile([P, PACK, P], F32)
-        nc.vector.tensor_copy(out=inv_l_rows[:], in_=repeat_on_all_partitions(inv_l, PACK)[:])
+        inv_l_rows = repeat_on_all_partitions(inv_l, PACK)
 
         poly_scale = keep.tile([P, 1], F32)
         poly_bias = keep.tile([P, 1], F32)
@@ -91,27 +96,27 @@ def tile_matern52_s_kernel(tc, X1, X2, c, l, out):
         sq2_rows = keep.tile([P, X2_TILES, P], F32)
         s_all = keep.tile([P, X1_TILES, N2], F32)
         w_all = keep.tile([P, X1_TILES, N2], F32)
+        result_all = keep.tile([P, X1_TILES, N2], F32)
 
-        def points(j):
-            if j < X2_TILES:
-                return x2_sb[:, j, :], b_codes[:, j, :], b_scales[:, j, :], sq2[:, j : j + 1]
-            i = j - X2_TILES
-            return x1_sb[:, i, :], a_codes[:, i, :], a_scales[:, i, :], sq1[:, i : i + 1]
+        x_of = [x2_sb[:, j, :] for j in range(X2_TILES)] + [x1_sb[:, i, :] for i in range(X1_TILES)]
+        codes_of = [b_codes[:, j, :] for j in range(X2_TILES)] + [a_codes[:, i, :] for i in range(X1_TILES)]
+        scales_of = [b_scales[:, j, :] for j in range(X2_TILES)] + [a_scales[:, i, :] for i in range(X1_TILES)]
+        sq_of = [sq2[:, j : j + 1] for j in range(X2_TILES)] + [sq1[:, i : i + 1] for i in range(X1_TILES)]
 
-        scaled, flipped, grouped, cross, part, d2 = {}, {}, {}, {}, {}, {}
+        scaled, flipped, grouped, cross, part, d2, rows_of = {}, {}, {}, {}, {}, {}, {}
 
         def scale(j):
-            scaled[j] = work.tile([P, PACK, P], F32, name="scaled", tag="scaled")
+            scaled[j] = scaled_pool.tile([P, PACK, P], F32, name="scaled", tag="scaled")
             nc.vector.tensor_tensor(
                 out=scaled[j][:],
-                in0=points(j)[0].rearrange("n (p t) -> n t p", t=PACK),
+                in0=x_of[j].rearrange("n (p t) -> n t p", t=PACK),
                 in1=inv_l_rows[:],
                 op=ALU.mult,
             )
 
         def sum_squares(j):
             squares = work.tile([P, PACK, P], F32, name="squares", tag="squares")
-            nc.scalar.activation(out=squares[:], in_=scaled[j][:], func=ACT.Square, accum_out=points(j)[3])
+            nc.scalar.activation(out=squares[:], in_=scaled[j][:], func=ACT.Square, accum_out=sq_of[j])
 
         def flip(j):
             flipped[j] = psum_flip.tile([P, PACK, P], F32, name="flipped", tag="flipped")
@@ -122,19 +127,16 @@ def tile_matern52_s_kernel(tc, X1, X2, c, l, out):
             grouped[j] = work.tile([P, P, PACK], BF16, name="grouped", tag="grouped", align_bytes=64)
             planes = flipped[j][:].rearrange("p t n -> p n t")
             if j % 2 == 0:
-                nc.vector.tensor_copy(out=grouped[j][:], in_=planes)
-            else:
                 nc.scalar.copy(out=grouped[j][:], in_=planes)
+            else:
+                nc.vector.tensor_copy(out=grouped[j][:], in_=planes)
 
         def quantise(j):
             nc.vector.quantize_mx(
-                out=points(j)[1].bitcast(FP8X4),
-                scales=points(j)[2],
+                out=codes_of[j].bitcast(FP8X4),
+                scales=scales_of[j],
                 in_=grouped[j][:].rearrange("p n t -> p (n t)"),
             )
-
-        def spread_sq2():
-            nc.scalar.copy(out=sq2_rows[:], in_=repeat_on_all_partitions(sq2, X2_TILES)[:])
 
         def multiply(i):
             cross[i] = psum_cross.tile([P, N2], F32, name="cross", tag="cross")
@@ -176,30 +178,36 @@ def tile_matern52_s_kernel(tc, X1, X2, c, l, out):
         def decay_finish_store(i):
             decay = work.tile([P, N2], F32, name="decay", tag="decay")
             nc.scalar.activation(out=decay[:], in_=s_all[:, i, :], func=ACT.Exp, scale=-1.0)
-            result = work.tile([P, N2], F32, name="result", tag="result")
             nc.vector.scalar_tensor_tensor(
-                out=result[:], in0=w_all[:, i, :], scalar=poly_add[:], in1=decay[:], op0=ALU.add, op1=ALU.mult
+                out=result_all[:, i, :],
+                in0=w_all[:, i, :],
+                scalar=poly_add[:],
+                in1=decay[:],
+                op0=ALU.add,
+                op1=ALU.mult,
             )
-            nc.sync.dma_start(out=out_view[:, i, :], in_=result[:])
+            nc.sync.dma_start(out=out_view[:, i, :], in_=result_all[:, i, :])
 
         def due(stage, index, count):
             if 0 <= index < count:
                 stage(index)
 
-        X1_LAG = X2_TILES + 3
-        for k in range(X1_TILES + X1_LAG + 1):
-            due(multiply, k - X1_LAG, X1_TILES)
+        for k in range(POINT_TILES + ROOT_LAG):
+            i = k - X2_TILES
+            due(multiply, i - MULTIPLY_LAG, X1_TILES)
             if k == X2_TILES + 1:
-                spread_sq2()
+                rows_of["sq2"] = repeat_on_all_partitions(sq2, X2_TILES)
             due(scale, k, POINT_TILES)
-            due(regroup, k - 1, POINT_TILES)
+            due(regroup, k - REGROUP_LAG, POINT_TILES)
             due(flip, k, POINT_TILES)
-            due(bracket, k - X1_LAG, X1_TILES)
-            due(root, k - X1_LAG - 1, X1_TILES)
-            due(quantise, k - 2, POINT_TILES)
+            due(bracket, i - MULTIPLY_LAG, X1_TILES)
+            due(root, i - ROOT_LAG, X1_TILES)
+            due(quantise, k - QUANTISE_LAG, POINT_TILES)
             due(sum_squares, k, POINT_TILES)
-            due(clamp, k - X1_LAG, X1_TILES)
-            due(polynomial, k - X1_LAG - 1, X1_TILES)
+            due(clamp, i - MULTIPLY_LAG, X1_TILES)
+            due(polynomial, i - ROOT_LAG, X1_TILES)
+            if k == X2_TILES + 2:
+                nc.scalar.copy(out=sq2_rows[:], in_=rows_of["sq2"][:])
 
         for i in range(X1_TILES):
             decay_finish_store(i)

@@ -25,6 +25,7 @@ REGROUP_LAG = 2
 QUANTISE_LAG = 3
 MULTIPLY_LAG = 5
 ROOT_LAG = 6
+VECTOR_POLYNOMIALS = 3
 
 FLOPS = 2 * N1 * N2 * D
 
@@ -103,7 +104,7 @@ def tile_matern52_s_kernel(tc, X1, X2, c, l, out):
         scales_of = [b_scales[:, j, :] for j in range(X2_TILES)] + [a_scales[:, i, :] for i in range(X1_TILES)]
         sq_of = [sq2[:, j : j + 1] for j in range(X2_TILES)] + [sq1[:, i : i + 1] for i in range(X1_TILES)]
 
-        scaled, flipped, grouped, cross, part, d2, rows_of = {}, {}, {}, {}, {}, {}, {}
+        scaled, flipped, grouped, cross, part, d2, rows_of, shifted = {}, {}, {}, {}, {}, {}, {}, {}
 
         def scale(j):
             scaled[j] = scaled_pool.tile([P, PACK, P], F32, name="scaled", tag="scaled")
@@ -175,6 +176,20 @@ def tile_matern52_s_kernel(tc, X1, X2, c, l, out):
                 out=w_all[:, i, :], in_=s_all[:, i, :], func=ACT.Square, scale=poly_scale[:], bias=poly_bias[:]
             )
 
+        def shift_on_vector(i):
+            shifted[i] = work.tile([P, N2], F32, name="shifted", tag="shifted")
+            nc.vector.tensor_scalar(
+                out=shifted[i][:],
+                in0=s_all[:, i, :],
+                scalar1=poly_scale[:],
+                scalar2=poly_bias[:],
+                op0=ALU.mult,
+                op1=ALU.add,
+            )
+
+        def square_on_vector(i):
+            nc.vector.tensor_tensor(out=w_all[:, i, :], in0=shifted[i][:], in1=shifted[i][:], op=ALU.mult)
+
         def decay_finish_store(i):
             decay = work.tile([P, N2], F32, name="decay", tag="decay")
             nc.scalar.activation(out=decay[:], in_=s_all[:, i, :], func=ACT.Exp, scale=-1.0)
@@ -205,9 +220,14 @@ def tile_matern52_s_kernel(tc, X1, X2, c, l, out):
             due(quantise, k - QUANTISE_LAG, POINT_TILES)
             due(sum_squares, k, POINT_TILES)
             due(clamp, i - MULTIPLY_LAG, X1_TILES)
-            due(polynomial, i - ROOT_LAG, X1_TILES)
+            due(polynomial, i - ROOT_LAG, X1_TILES - VECTOR_POLYNOMIALS)
             if k == X2_TILES + 2:
                 nc.scalar.copy(out=sq2_rows[:], in_=rows_of["sq2"][:])
+
+        for i in range(X1_TILES - VECTOR_POLYNOMIALS, X1_TILES):
+            shift_on_vector(i)
+        for i in range(X1_TILES - VECTOR_POLYNOMIALS, X1_TILES):
+            square_on_vector(i)
 
         for i in range(X1_TILES):
             decay_finish_store(i)

@@ -25,7 +25,7 @@ REGROUP_LAG = 2
 QUANTISE_LAG = 3
 MULTIPLY_LAG = 5
 ROOT_LAG = 6
-VECTOR_POLYNOMIALS = 3
+VECTOR_POLYNOMIALS = 4
 
 FLOPS = 2 * N1 * N2 * D
 
@@ -127,10 +127,10 @@ def tile_matern52_s_kernel(tc, X1, X2, c, l, out):
         def regroup(j):
             grouped[j] = work.tile([P, P, PACK], BF16, name="grouped", tag="grouped", align_bytes=64)
             planes = flipped[j][:].rearrange("p t n -> p n t")
-            if j % 2 == 0:
-                nc.scalar.copy(out=grouped[j][:], in_=planes)
-            else:
+            if j % 3 == 0:
                 nc.vector.tensor_copy(out=grouped[j][:], in_=planes)
+            else:
+                nc.scalar.copy(out=grouped[j][:], in_=planes)
 
         def quantise(j):
             nc.vector.quantize_mx(
@@ -177,7 +177,7 @@ def tile_matern52_s_kernel(tc, X1, X2, c, l, out):
             )
 
         def shift_on_vector(i):
-            shifted[i] = work.tile([P, N2], F32, name="shifted", tag="shifted")
+            shifted[i] = work.tile([P, N2], F32, name="shifted", tag="shifted", bufs=VECTOR_POLYNOMIALS)
             nc.vector.tensor_scalar(
                 out=shifted[i][:],
                 in0=s_all[:, i, :],

@@ -25,7 +25,7 @@ REGROUP_LAG = 2
 QUANTISE_LAG = 3
 MULTIPLY_LAG = 5
 ROOT_LAG = 6
-VECTOR_POLYNOMIALS = 4
+VECTOR_POLYNOMIALS = 5
 
 FLOPS = 2 * N1 * N2 * D
 
@@ -44,7 +44,7 @@ def tile_matern52_s_kernel(tc, X1, X2, c, l, out):
         l_sb = keep.tile([P, PACK], BF16)
         nc.sync.dma_start(out=l_sb[:], in_=l.rearrange("(p t) -> p t", t=PACK))
         c_sb = keep.tile([P, 1], BF16)
-        nc.scalar.dma_start(out=c_sb[:], in_=c.partition_broadcast(P))
+        nc.sync.dma_start(out=c_sb[:], in_=c.partition_broadcast(P))
         x2_sb = keep.tile([P, X2_TILES, D], BF16)
         x2_view = X2.rearrange("(j p) d -> p j d", p=P)
         for j in range(0, X2_TILES, LOAD_TILES):
@@ -72,21 +72,30 @@ def tile_matern52_s_kernel(tc, X1, X2, c, l, out):
         nc.vector.reciprocal(out=inv_l[:], in_=l_sb[:])
         inv_l_rows = repeat_on_all_partitions(inv_l, PACK)
 
-        poly_scale = keep.tile([P, 1], F32)
-        poly_bias = keep.tile([P, 1], F32)
-        c_f32 = keep.tile([P, 1], F32)
-        c_quarter = keep.tile([P, 1], F32)
-        poly_add = keep.tile([P, 1], F32)
-        for scalar_tile, factor in (
-            (poly_scale, 1.0 / math.sqrt(3.0)),
-            (poly_bias, 1.5 / math.sqrt(3.0)),
-            (c_f32, 1.0),
-            (c_quarter, 0.25),
-        ):
-            nc.gpsimd.tensor_scalar(
-                out=scalar_tile[:], in0=c_sb[:], scalar1=factor, scalar2=0.0, op0=ALU.mult, op1=ALU.add
+        c_abs = keep.tile([P, 1], F32)
+        nc.vector.scalar_tensor_tensor(
+            out=c_abs[:], in0=c_sb[:], scalar=-1.0, in1=c_sb[:], op0=ALU.mult, op1=ALU.max
+        )
+        k_sb = keep.tile([P, 1], F32)
+        nc.vector.tensor_scalar(
+            out=k_sb[:], in0=c_abs[:], scalar1=1e-15, scalar2=1.0 / math.sqrt(3.0), op0=ALU.max, op1=ALU.mult
+        )
+        inv_k = keep.tile([P, 1], F32)
+        nc.vector.reciprocal(out=inv_k[:], in_=k_sb[:])
+        kk_5 = keep.tile([P, 1], F32)
+        kk_3 = keep.tile([P, 1], F32)
+        kk_075 = keep.tile([P, 1], F32)
+        k_15 = keep.tile([P, 1], F32)
+        k_30 = keep.tile([P, 1], F32)
+        exp_scale = keep.tile([P, 1], F32)
+        for square_tile, factor in ((kk_5, 5.0), (kk_3, 3.0), (kk_075, 0.75)):
+            nc.vector.tensor_scalar(
+                out=square_tile[:], in0=k_sb[:], scalar1=k_sb[:], scalar2=factor, op0=ALU.mult, op1=ALU.mult
             )
-        nc.gpsimd.tensor_tensor(out=poly_add[:], in0=c_quarter[:], in1=c_f32[:], op=ALU.mult)
+        for multiple, source, factor in ((k_15, k_sb, 1.5), (k_30, k_sb, 3.0), (exp_scale, inv_k, -1.0)):
+            nc.vector.tensor_scalar(
+                out=multiple[:], in0=source[:], scalar1=factor, scalar2=0.0, op0=ALU.mult, op1=ALU.add
+            )
 
         a_codes = keep.tile([P, X1_TILES, P], U32, align_bytes=64)
         a_scales = keep.tile([P, X1_TILES, P], U8, align_bytes=64)
@@ -169,39 +178,36 @@ def tile_matern52_s_kernel(tc, X1, X2, c, l, out):
             )
 
         def root(i):
-            nc.scalar.activation(out=s_all[:, i, :], in_=d2[i][:], func=ACT.Sqrt, scale=5.0)
+            nc.scalar.activation(out=s_all[:, i, :], in_=d2[i][:], func=ACT.Sqrt, scale=kk_5[:])
 
         def polynomial(i):
             nc.scalar.activation(
-                out=w_all[:, i, :], in_=s_all[:, i, :], func=ACT.Square, scale=poly_scale[:], bias=poly_bias[:]
+                out=w_all[:, i, :], in_=s_all[:, i, :], func=ACT.Square, bias=k_15[:]
             )
 
-        def shift_on_vector(i):
-            shifted[i] = work.tile([P, N2], F32, name="shifted", tag="shifted", bufs=VECTOR_POLYNOMIALS)
-            nc.vector.tensor_scalar(
-                out=shifted[i][:],
-                in0=s_all[:, i, :],
-                scalar1=poly_scale[:],
-                scalar2=poly_bias[:],
-                op0=ALU.mult,
-                op1=ALU.add,
-            )
-
-        def square_on_vector(i):
-            nc.vector.tensor_tensor(out=w_all[:, i, :], in0=shifted[i][:], in1=shifted[i][:], op=ALU.mult)
-
-        def decay_finish_store(i):
-            decay = work.tile([P, N2], F32, name="decay", tag="decay")
-            nc.scalar.activation(out=decay[:], in_=s_all[:, i, :], func=ACT.Exp, scale=-1.0)
+        def vector_polynomial(i):
             nc.vector.scalar_tensor_tensor(
-                out=result_all[:, i, :],
-                in0=w_all[:, i, :],
-                scalar=poly_add[:],
-                in1=decay[:],
+                out=w_all[:, i, :],
+                in0=s_all[:, i, :],
+                scalar=k_30[:],
+                in1=s_all[:, i, :],
                 op0=ALU.add,
                 op1=ALU.mult,
             )
-            nc.sync.dma_start(out=out_view[:, i, :], in_=result_all[:, i, :])
+
+        def decay_finish_store(i, first, last):
+            decay = work.tile([P, N2], F32, name="decay", tag="decay")
+            columns = slice(first, last)
+            nc.scalar.activation(out=decay[:, columns], in_=s_all[:, i, columns], func=ACT.Exp, scale=exp_scale[:])
+            nc.vector.scalar_tensor_tensor(
+                out=result_all[:, i, columns],
+                in0=w_all[:, i, columns],
+                scalar=kk_075[:] if i < X1_TILES - VECTOR_POLYNOMIALS else kk_3[:],
+                in1=decay[:, columns],
+                op0=ALU.add,
+                op1=ALU.mult,
+            )
+            nc.sync.dma_start(out=out_view[:, i, columns], in_=result_all[:, i, columns])
 
         def due(stage, index, count):
             if 0 <= index < count:
@@ -225,9 +231,9 @@ def tile_matern52_s_kernel(tc, X1, X2, c, l, out):
                 nc.scalar.copy(out=sq2_rows[:], in_=rows_of["sq2"][:])
 
         for i in range(X1_TILES - VECTOR_POLYNOMIALS, X1_TILES):
-            shift_on_vector(i)
-        for i in range(X1_TILES - VECTOR_POLYNOMIALS, X1_TILES):
-            square_on_vector(i)
+            vector_polynomial(i)
 
-        for i in range(X1_TILES):
-            decay_finish_store(i)
+        for i in range(X1_TILES - 1):
+            decay_finish_store(i, 0, N2)
+        for half in range(2):
+            decay_finish_store(X1_TILES - 1, half * N2 // 2, (half + 1) * N2 // 2)

@@ -24,7 +24,11 @@ LOAD_TILES = 2
 REGROUP_LAG = 2
 QUANTISE_LAG = 3
 MULTIPLY_LAG = 5
-ROOT_LAG = 6
+ROOT_LAG = 7
+GP = (4,6,8,10,11)
+QB = 7
+CLAMP_G = ()
+VRG = lambda j: j % 2 == 1
 VECTOR_POLYNOMIALS = 5
 
 FLOPS = 2 * N1 * N2 * D
@@ -34,8 +38,8 @@ def tile_matern52_s_kernel(tc, X1, X2, c, l, out):
     nc = tc.nc
     with ExitStack() as stack:
         keep = stack.enter_context(tc.tile_pool(name="keep", bufs=1))
-        work = stack.enter_context(tc.tile_pool(name="work", bufs=3))
-        scaled_pool = stack.enter_context(tc.tile_pool(name="scaled_pool", bufs=4))
+        work = stack.enter_context(tc.tile_pool(name="work", bufs=4))
+        scaled_pool = stack.enter_context(tc.tile_pool(name="scaled_pool", bufs=12))
         psum_rows = stack.enter_context(tc.psum_pool(name="psum_rows", bufs=2))
         psum_flip = stack.enter_context(tc.psum_pool(name="psum_flip", bufs=4))
         psum_cross = stack.enter_context(tc.psum_pool(name="psum_cross", bufs=2))
@@ -71,6 +75,9 @@ def tile_matern52_s_kernel(tc, X1, X2, c, l, out):
         inv_l = keep.tile([P, PACK], F32)
         nc.vector.reciprocal(out=inv_l[:], in_=l_sb[:])
         inv_l_rows = repeat_on_all_partitions(inv_l, PACK)
+        inv_l_copy = repeat_on_all_partitions(inv_l, PACK)
+        inv_l_sb = keep.tile([P, PACK, P], F32)
+        nc.scalar.copy(out=inv_l_sb[:], in_=inv_l_copy[:])
 
         c_abs = keep.tile([P, 1], F32)
         nc.vector.scalar_tensor_tensor(
@@ -109,19 +116,15 @@ def tile_matern52_s_kernel(tc, X1, X2, c, l, out):
         result_all = keep.tile([P, X1_TILES, N2], F32)
 
         x_of = [x2_sb[:, j, :] for j in range(X2_TILES)] + [x1_sb[:, i, :] for i in range(X1_TILES)]
-        codes_of = [b_codes[:, j, :] for j in range(X2_TILES)] + [a_codes[:, i, :] for i in range(X1_TILES)]
-        scales_of = [b_scales[:, j, :] for j in range(X2_TILES)] + [a_scales[:, i, :] for i in range(X1_TILES)]
         sq_of = [sq2[:, j : j + 1] for j in range(X2_TILES)] + [sq1[:, i : i + 1] for i in range(X1_TILES)]
 
         scaled, flipped, grouped, cross, part, d2, rows_of, shifted = {}, {}, {}, {}, {}, {}, {}, {}
 
         def scale(j):
             scaled[j] = scaled_pool.tile([P, PACK, P], F32, name="scaled", tag="scaled")
-            nc.vector.tensor_tensor(
-                out=scaled[j][:],
-                in0=x_of[j].rearrange("n (p t) -> n t p", t=PACK),
-                in1=inv_l_rows[:],
-                op=ALU.mult,
+            engine, rows = (nc.gpsimd, inv_l_sb) if j in GP else (nc.vector, inv_l_rows)
+            engine.tensor_tensor(
+                out=scaled[j][:], in0=x_of[j].rearrange("n (p t) -> n t p", t=PACK), in1=rows[:], op=ALU.mult
             )
 
         def sum_squares(j):
@@ -134,18 +137,30 @@ def tile_matern52_s_kernel(tc, X1, X2, c, l, out):
                 nc.tensor.transpose(flipped[j][:, t, :], scaled[j][:, t, :], ident[:])
 
         def regroup(j):
-            grouped[j] = work.tile([P, P, PACK], BF16, name="grouped", tag="grouped", align_bytes=64)
-            planes = flipped[j][:].rearrange("p t n -> p n t")
-            if j % 3 == 0:
-                nc.vector.tensor_copy(out=grouped[j][:], in_=planes)
+            if j == 0:
+                grouped["x2"] = keep.tile([P, X2_TILES, P, PACK], BF16, name="grouped_x2", align_bytes=64)
+            if j < X2_TILES:
+                grouped[j] = grouped["x2"][:, j, :, :]
             else:
-                nc.scalar.copy(out=grouped[j][:], in_=planes)
+                grouped[j] = work.tile([P, P, PACK], BF16, name="grouped", tag="grouped", align_bytes=64)
+            planes = flipped[j][:].rearrange("p t n -> p n t")
+            if VRG(j):
+                nc.vector.tensor_copy(out=grouped[j] if j < X2_TILES else grouped[j][:], in_=planes)
+            else:
+                nc.scalar.copy(out=grouped[j] if j < X2_TILES else grouped[j][:], in_=planes)
 
-        def quantise(j):
+        def quantise_x2():
             nc.vector.quantize_mx(
-                out=codes_of[j].bitcast(FP8X4),
-                scales=scales_of[j],
-                in_=grouped[j][:].rearrange("p n t -> p (n t)"),
+                out=b_codes[:].rearrange("p j n -> p (j n)").bitcast(FP8X4),
+                scales=b_scales[:].rearrange("p j n -> p (j n)"),
+                in_=grouped["x2"][:].rearrange("p j n t -> p (j n t)"),
+            )
+
+        def quantise_x1(i):
+            nc.vector.quantize_mx(
+                out=a_codes[:, i, :].bitcast(FP8X4),
+                scales=a_scales[:, i, :],
+                in_=grouped[X2_TILES + i][:].rearrange("p n t -> p (n t)"),
             )
 
         def multiply(i):
@@ -173,7 +188,8 @@ def tile_matern52_s_kernel(tc, X1, X2, c, l, out):
 
         def clamp(i):
             d2[i] = work.tile([P, N2], F32, name="d2", tag="d2")
-            nc.vector.tensor_scalar(
+            engine = nc.gpsimd if i in CLAMP_G else nc.vector
+            engine.tensor_scalar(
                 out=d2[i][:], in0=part[i][:], scalar1=sq1[:, i : i + 1], scalar2=0.0, op0=ALU.add, op1=ALU.max
             )
 
@@ -223,7 +239,9 @@ def tile_matern52_s_kernel(tc, X1, X2, c, l, out):
             due(flip, k, POINT_TILES)
             due(bracket, i - MULTIPLY_LAG, X1_TILES)
             due(root, i - ROOT_LAG, X1_TILES)
-            due(quantise, k - QUANTISE_LAG, POINT_TILES)
+            if k == QB:
+                quantise_x2()
+            due(quantise_x1, i - QUANTISE_LAG, X1_TILES)
             due(sum_squares, k, POINT_TILES)
             due(clamp, i - MULTIPLY_LAG, X1_TILES)
             due(polynomial, i - ROOT_LAG, X1_TILES - VECTOR_POLYNOMIALS)

@@ -25,10 +25,10 @@ REGROUP_LAG = 2
 QUANTISE_LAG = 3
 MULTIPLY_LAG = 5
 ROOT_LAG = 7
-GP = (4,6,8,10,11)
+GP = (6,7,8,9,10,11)
 QB = 7
 CLAMP_G = ()
-VRG = lambda j: j % 2 == 1
+VRG = lambda j: 2 <= j < 8
 VECTOR_POLYNOMIALS = 5
 
 FLOPS = 2 * N1 * N2 * D

@@ -25,11 +25,11 @@ REGROUP_LAG = 2
 QUANTISE_LAG = 3
 MULTIPLY_LAG = 5
 ROOT_LAG = 7
-GP = (6,7,8,9,10,11)
+GP = (7,8,9,10,11)
 QB = 7
 CLAMP_G = ()
 VRG = lambda j: 2 <= j < 8
-VECTOR_POLYNOMIALS = 5
+VECTOR_POLYNOMIALS = 6
 
 FLOPS = 2 * N1 * N2 * D
 
@@ -79,30 +79,33 @@ def tile_matern52_s_kernel(tc, X1, X2, c, l, out):
         inv_l_sb = keep.tile([P, PACK, P], F32)
         nc.scalar.copy(out=inv_l_sb[:], in_=inv_l_copy[:])
 
-        c_abs = keep.tile([P, 1], F32)
-        nc.vector.scalar_tensor_tensor(
-            out=c_abs[:], in0=c_sb[:], scalar=-1.0, in1=c_sb[:], op0=ALU.mult, op1=ALU.max
-        )
+        square_factors = keep.tile([P, 3], F32)
+        for column, factor in enumerate((5.0, 3.0, 0.75)):
+            nc.vector.memset(square_factors[:, column : column + 1], factor)
+        factors = keep.tile([P, 3], F32)
+        for column, factor in enumerate((1.5, 3.0, -1.0)):
+            nc.vector.memset(factors[:, column : column + 1], factor)
+        c_pos = keep.tile([P, 1], F32)
+        c_neg = keep.tile([P, 1], F32)
         k_sb = keep.tile([P, 1], F32)
-        nc.vector.tensor_scalar(
-            out=k_sb[:], in0=c_abs[:], scalar1=1e-15, scalar2=1.0 / math.sqrt(3.0), op0=ALU.max, op1=ALU.mult
+        for signed, factor in ((c_pos, 1.0 / math.sqrt(3.0)), (c_neg, -1.0 / math.sqrt(3.0))):
+            nc.gpsimd.tensor_scalar(
+                out=signed[:], in0=c_sb[:], scalar1=factor, scalar2=0.0, op0=ALU.mult, op1=ALU.add
+            )
+        nc.gpsimd.tensor_scalar(
+            out=k_sb[:], in0=c_neg[:], scalar1=c_pos[:], scalar2=1e-15, op0=ALU.max, op1=ALU.max
         )
-        inv_k = keep.tile([P, 1], F32)
-        nc.vector.reciprocal(out=inv_k[:], in_=k_sb[:])
-        kk_5 = keep.tile([P, 1], F32)
-        kk_3 = keep.tile([P, 1], F32)
-        kk_075 = keep.tile([P, 1], F32)
-        k_15 = keep.tile([P, 1], F32)
-        k_30 = keep.tile([P, 1], F32)
+        kk_all = keep.tile([P, 3], F32)
+        nc.gpsimd.tensor_scalar(
+            out=kk_all[:], in0=square_factors[:], scalar1=k_sb[:], scalar2=k_sb[:], op0=ALU.mult, op1=ALU.mult
+        )
+        k_all = keep.tile([P, 3], F32)
+        nc.gpsimd.tensor_scalar(
+            out=k_all[:], in0=factors[:], scalar1=k_sb[:], scalar2=0.0, op0=ALU.mult, op1=ALU.add
+        )
+        kk_5, kk_3, kk_075 = (kk_all[:, column : column + 1] for column in range(3))
+        k_15, k_30, k_minus = (k_all[:, column : column + 1] for column in range(3))
         exp_scale = keep.tile([P, 1], F32)
-        for square_tile, factor in ((kk_5, 5.0), (kk_3, 3.0), (kk_075, 0.75)):
-            nc.vector.tensor_scalar(
-                out=square_tile[:], in0=k_sb[:], scalar1=k_sb[:], scalar2=factor, op0=ALU.mult, op1=ALU.mult
-            )
-        for multiple, source, factor in ((k_15, k_sb, 1.5), (k_30, k_sb, 3.0), (exp_scale, inv_k, -1.0)):
-            nc.vector.tensor_scalar(
-                out=multiple[:], in0=source[:], scalar1=factor, scalar2=0.0, op0=ALU.mult, op1=ALU.add
-            )
 
         a_codes = keep.tile([P, X1_TILES, P], U32, align_bytes=64)
         a_scales = keep.tile([P, X1_TILES, P], U8, align_bytes=64)
@@ -194,18 +197,18 @@ def tile_matern52_s_kernel(tc, X1, X2, c, l, out):
             )
 
         def root(i):
-            nc.scalar.activation(out=s_all[:, i, :], in_=d2[i][:], func=ACT.Sqrt, scale=kk_5[:])
+            nc.scalar.activation(out=s_all[:, i, :], in_=d2[i][:], func=ACT.Sqrt, scale=kk_5)
 
         def polynomial(i):
             nc.scalar.activation(
-                out=w_all[:, i, :], in_=s_all[:, i, :], func=ACT.Square, bias=k_15[:]
+                out=w_all[:, i, :], in_=s_all[:, i, :], func=ACT.Square, bias=k_15
             )
 
         def vector_polynomial(i):
             nc.vector.scalar_tensor_tensor(
                 out=w_all[:, i, :],
                 in0=s_all[:, i, :],
-                scalar=k_30[:],
+                scalar=k_30,
                 in1=s_all[:, i, :],
                 op0=ALU.add,
                 op1=ALU.mult,
@@ -218,7 +221,7 @@ def tile_matern52_s_kernel(tc, X1, X2, c, l, out):
             nc.vector.scalar_tensor_tensor(
                 out=result_all[:, i, columns],
                 in0=w_all[:, i, columns],
-                scalar=kk_075[:] if i < X1_TILES - VECTOR_POLYNOMIALS else kk_3[:],
+                scalar=kk_075 if i < X1_TILES - VECTOR_POLYNOMIALS else kk_3,
                 in1=decay[:, columns],
                 op0=ALU.add,
                 op1=ALU.mult,
@@ -229,25 +232,30 @@ def tile_matern52_s_kernel(tc, X1, X2, c, l, out):
             if 0 <= index < count:
                 stage(index)
 
-        for k in range(POINT_TILES + ROOT_LAG):
+        for k in range(POINT_TILES + ROOT_LAG + 4):
             i = k - X2_TILES
-            due(multiply, i - MULTIPLY_LAG, X1_TILES)
+            now = [tile for tile in range(X1_TILES) if min(tile + MULTIPLY_LAG, X1_TILES + QUANTISE_LAG) == i]
+            for tile in now:
+                multiply(tile)
             if k == X2_TILES + 1:
                 rows_of["sq2"] = repeat_on_all_partitions(sq2, X2_TILES)
             due(scale, k, POINT_TILES)
             due(regroup, k - REGROUP_LAG, POINT_TILES)
             due(flip, k, POINT_TILES)
-            due(bracket, i - MULTIPLY_LAG, X1_TILES)
+            for tile in now:
+                bracket(tile)
             due(root, i - ROOT_LAG, X1_TILES)
             if k == QB:
                 quantise_x2()
             due(quantise_x1, i - QUANTISE_LAG, X1_TILES)
             due(sum_squares, k, POINT_TILES)
-            due(clamp, i - MULTIPLY_LAG, X1_TILES)
-            due(polynomial, i - ROOT_LAG, X1_TILES - VECTOR_POLYNOMIALS)
+            for tile in now:
+                clamp(tile)
+            due(polynomial, i - ROOT_LAG - 1, X1_TILES - VECTOR_POLYNOMIALS)
             if k == X2_TILES + 2:
                 nc.scalar.copy(out=sq2_rows[:], in_=rows_of["sq2"][:])
 
+        nc.vector.reciprocal(out=exp_scale[:], in_=k_minus)
         for i in range(X1_TILES - VECTOR_POLYNOMIALS, X1_TILES):
             vector_polynomial(i)
 

@@ -18,18 +18,9 @@ N1, N2, D = 1024, 512, 512
 assert D == P * PACK
 X1_TILES = N1 // P
 X2_TILES = N2 // P
-POINT_TILES = X2_TILES + X1_TILES
-LOAD_TILES = 2
-
-REGROUP_LAG = 2
-QUANTISE_LAG = 3
-MULTIPLY_LAG = 5
-ROOT_LAG = 7
-GP = (7,8,9,10,11)
-QB = 7
-CLAMP_G = ()
-VRG = lambda j: 2 <= j < 8
-VECTOR_POLYNOMIALS = 6
+X1_PAIRS = X1_TILES // 2
+PAIR = 2 * P
+SCALAR_POLYNOMIALS = 2
 
 FLOPS = 2 * N1 * N2 * D
 
@@ -39,25 +30,29 @@ def tile_matern52_s_kernel(tc, X1, X2, c, l, out):
     with ExitStack() as stack:
         keep = stack.enter_context(tc.tile_pool(name="keep", bufs=1))
         work = stack.enter_context(tc.tile_pool(name="work", bufs=4))
-        scaled_pool = stack.enter_context(tc.tile_pool(name="scaled_pool", bufs=12))
-        psum_rows = stack.enter_context(tc.psum_pool(name="psum_rows", bufs=2))
         psum_flip = stack.enter_context(tc.psum_pool(name="psum_flip", bufs=4))
+        psum_rows = stack.enter_context(tc.psum_pool(name="psum_rows", bufs=2))
         psum_cross = stack.enter_context(tc.psum_pool(name="psum_cross", bufs=2))
         stack.enter_context(tc.manual_schedule())
 
-        l_sb = keep.tile([P, PACK], BF16)
-        nc.sync.dma_start(out=l_sb[:], in_=l.rearrange("(p t) -> p t", t=PACK))
+        l_sb = keep.tile([P, 2, 2], BF16)
+        nc.sync.dma_start(out=l_sb[:], in_=l.rearrange("(u p e) -> p u e", u=2, e=2))
         c_sb = keep.tile([P, 1], BF16)
-        nc.sync.dma_start(out=c_sb[:], in_=c.partition_broadcast(P))
+        nc.scalar.dma_start(out=c_sb[:], in_=c.partition_broadcast(P))
         x2_sb = keep.tile([P, X2_TILES, D], BF16)
         x2_view = X2.rearrange("(j p) d -> p j d", p=P)
-        for j in range(0, X2_TILES, LOAD_TILES):
-            nc.sync.dma_start(out=x2_sb[:, j : j + LOAD_TILES, :], in_=x2_view[:, j : j + LOAD_TILES, :])
         x1_sb = keep.tile([P, X1_TILES, D], BF16)
         x1_view = X1.rearrange("(p i) d -> p i d", i=X1_TILES)
         out_view = out.rearrange("(p i) m -> p i m", i=X1_TILES)
-        for i in range(0, X1_TILES, LOAD_TILES):
-            nc.sync.dma_start(out=x1_sb[:, i : i + LOAD_TILES, :], in_=x1_view[:, i : i + LOAD_TILES, :])
+        for x_sb, view, k in (
+            (x2_sb, x2_view, 0),
+            (x1_sb, x1_view, 0),
+            (x2_sb, x2_view, 1),
+            (x1_sb, x1_view, 1),
+            (x1_sb, x1_view, 2),
+            (x1_sb, x1_view, 3),
+        ):
+            nc.sync.dma_start(out=x_sb[:, 2 * k : 2 * k + 2, :], in_=view[:, 2 * k : 2 * k + 2, :])
 
         ident = keep.tile([P, P], F32)
         make_identity(nc, ident[:])
@@ -65,6 +60,11 @@ def tile_matern52_s_kernel(tc, X1, X2, c, l, out):
         nc.vector.memset(one[:], 1.0)
         warm = keep.tile([P, 1], F32)
         nc.scalar.activation(out=warm[:], in_=one[:], func=ACT.Sqrt)
+        square_factors = keep.tile([P, 3], F32)
+        factors = keep.tile([P, 3], F32)
+        for column, (square_factor, factor) in enumerate(((5.0, 1.5), (3.0, 3.0), (0.75, -1.0))):
+            nc.vector.memset(square_factors[:, column : column + 1], square_factor)
+            nc.vector.memset(factors[:, column : column + 1], factor)
 
         def repeat_on_all_partitions(columns, count):
             rows = psum_rows.tile([P, count, P], F32, name="rows", tag="rows")
@@ -72,99 +72,101 @@ def tile_matern52_s_kernel(tc, X1, X2, c, l, out):
                 nc.tensor.transpose(rows[:, j, :], columns[:, j : j + 1].to_broadcast([P, P]), ident[:])
             return rows
 
-        inv_l = keep.tile([P, PACK], F32)
-        nc.vector.reciprocal(out=inv_l[:], in_=l_sb[:])
-        inv_l_rows = repeat_on_all_partitions(inv_l, PACK)
-        inv_l_copy = repeat_on_all_partitions(inv_l, PACK)
-        inv_l_sb = keep.tile([P, PACK, P], F32)
-        nc.scalar.copy(out=inv_l_sb[:], in_=inv_l_copy[:])
-
-        square_factors = keep.tile([P, 3], F32)
-        for column, factor in enumerate((5.0, 3.0, 0.75)):
-            nc.vector.memset(square_factors[:, column : column + 1], factor)
-        factors = keep.tile([P, 3], F32)
-        for column, factor in enumerate((1.5, 3.0, -1.0)):
-            nc.vector.memset(factors[:, column : column + 1], factor)
-        c_pos = keep.tile([P, 1], F32)
-        c_neg = keep.tile([P, 1], F32)
-        k_sb = keep.tile([P, 1], F32)
-        for signed, factor in ((c_pos, 1.0 / math.sqrt(3.0)), (c_neg, -1.0 / math.sqrt(3.0))):
-            nc.gpsimd.tensor_scalar(
-                out=signed[:], in0=c_sb[:], scalar1=factor, scalar2=0.0, op0=ALU.mult, op1=ALU.add
-            )
-        nc.gpsimd.tensor_scalar(
-            out=k_sb[:], in0=c_neg[:], scalar1=c_pos[:], scalar2=1e-15, op0=ALU.max, op1=ALU.max
-        )
-        kk_all = keep.tile([P, 3], F32)
-        nc.gpsimd.tensor_scalar(
-            out=kk_all[:], in0=square_factors[:], scalar1=k_sb[:], scalar2=k_sb[:], op0=ALU.mult, op1=ALU.mult
-        )
-        k_all = keep.tile([P, 3], F32)
-        nc.gpsimd.tensor_scalar(
-            out=k_all[:], in0=factors[:], scalar1=k_sb[:], scalar2=0.0, op0=ALU.mult, op1=ALU.add
-        )
-        kk_5, kk_3, kk_075 = (kk_all[:, column : column + 1] for column in range(3))
-        k_15, k_30, k_minus = (k_all[:, column : column + 1] for column in range(3))
-        exp_scale = keep.tile([P, 1], F32)
+        inv_l = keep.tile([P, 1, PACK], F32)
+        nc.vector.reciprocal(out=inv_l[:, 0, :], in_=l_sb[:].rearrange("p u e -> p (u e)"))
+        inv_l_rows = repeat_on_all_partitions(inv_l[:, 0, :], PACK)
+        inv_l_copy = repeat_on_all_partitions(inv_l[:, 0, :], PACK)
+        inv_l_sb = keep.tile([P, 2, P, 2], F32)
+        nc.scalar.copy(out=inv_l_sb[:], in_=inv_l_copy[:].rearrange("q (u e) p -> q u p e", u=2))
 
         a_codes = keep.tile([P, X1_TILES, P], U32, align_bytes=64)
         a_scales = keep.tile([P, X1_TILES, P], U8, align_bytes=64)
         b_codes = keep.tile([P, X2_TILES, P], U32, align_bytes=64)
         b_scales = keep.tile([P, X2_TILES, P], U8, align_bytes=64)
+        b_grouped = keep.tile([P, X2_TILES, P, PACK], BF16, align_bytes=64)
         sq1 = keep.tile([P, X1_TILES], F32)
         sq2 = keep.tile([P, X2_TILES], F32)
         sq2_rows = keep.tile([P, X2_TILES, P], F32)
-        s_all = keep.tile([P, X1_TILES, N2], F32)
+        sigma_all = keep.tile([P, X1_TILES, N2], F32)
         w_all = keep.tile([P, X1_TILES, N2], F32)
         result_all = keep.tile([P, X1_TILES, N2], F32)
+        c_abs = keep.tile([P, 1], F32)
+        k_sb = keep.tile([P, 1], F32)
+        kk_all = keep.tile([P, 3], F32)
+        k_all = keep.tile([P, 3], F32)
+        exp_scale = keep.tile([P, 1], F32)
+        kk_5, kk_3, kk_075 = (kk_all[:, column : column + 1] for column in range(3))
+        k_15, k_30, k_minus = (k_all[:, column : column + 1] for column in range(3))
 
-        x_of = [x2_sb[:, j, :] for j in range(X2_TILES)] + [x1_sb[:, i, :] for i in range(X1_TILES)]
-        sq_of = [sq2[:, j : j + 1] for j in range(X2_TILES)] + [sq1[:, i : i + 1] for i in range(X1_TILES)]
+        scaled, flipped, pairs, a_grouped, rows_of, cross, part, d2 = {}, {}, {}, {}, {}, {}, {}, {}
 
-        scaled, flipped, grouped, cross, part, d2, rows_of, shifted = {}, {}, {}, {}, {}, {}, {}, {}
-
-        def scale(j):
-            scaled[j] = scaled_pool.tile([P, PACK, P], F32, name="scaled", tag="scaled")
-            engine, rows = (nc.gpsimd, inv_l_sb) if j in GP else (nc.vector, inv_l_rows)
-            engine.tensor_tensor(
-                out=scaled[j][:], in0=x_of[j].rearrange("n (p t) -> n t p", t=PACK), in1=rows[:], op=ALU.mult
+        def scale_x2(j):
+            scaled["x2", j] = work.tile([P, PACK, P], F32, name="scaled_x2", tag="scaled_x2")
+            nc.vector.tensor_tensor(
+                out=scaled["x2", j][:].rearrange("n (u e) p -> n u e p", u=2),
+                in0=x2_sb[:, j, :].rearrange("n (u p e) -> n u e p", u=2, e=2),
+                in1=inv_l_rows[:].rearrange("q (u e) p -> q u e p", u=2),
+                op=ALU.mult,
             )
 
-        def sum_squares(j):
-            squares = work.tile([P, PACK, P], F32, name="squares", tag="squares")
-            nc.scalar.activation(out=squares[:], in_=scaled[j][:], func=ACT.Square, accum_out=sq_of[j])
-
-        def flip(j):
+        def flip_x2(j):
             flipped[j] = psum_flip.tile([P, PACK, P], F32, name="flipped", tag="flipped")
             for t in range(PACK):
-                nc.tensor.transpose(flipped[j][:, t, :], scaled[j][:, t, :], ident[:])
+                nc.tensor.transpose(flipped[j][:, t, :], scaled["x2", j][:, t, :], ident[:])
 
-        def regroup(j):
-            if j == 0:
-                grouped["x2"] = keep.tile([P, X2_TILES, P, PACK], BF16, name="grouped_x2", align_bytes=64)
-            if j < X2_TILES:
-                grouped[j] = grouped["x2"][:, j, :, :]
-            else:
-                grouped[j] = work.tile([P, P, PACK], BF16, name="grouped", tag="grouped", align_bytes=64)
-            planes = flipped[j][:].rearrange("p t n -> p n t")
-            if VRG(j):
-                nc.vector.tensor_copy(out=grouped[j] if j < X2_TILES else grouped[j][:], in_=planes)
-            else:
-                nc.scalar.copy(out=grouped[j] if j < X2_TILES else grouped[j][:], in_=planes)
+        def sum_squares(values, column):
+            squares = work.tile([P, D], F32, name="squares", tag="squares")
+            nc.scalar.activation(out=squares[:], in_=values, func=ACT.Square, accum_out=column)
+
+        def sum_squares_x2(j):
+            sum_squares(scaled["x2", j][:].rearrange("n t p -> n (t p)"), sq2[:, j : j + 1])
+
+        def regroup_x2(j):
+            nc.scalar.copy(out=b_grouped[:, j, :, :], in_=flipped[j][:].rearrange("p t n -> p n t"))
 
         def quantise_x2():
             nc.vector.quantize_mx(
                 out=b_codes[:].rearrange("p j n -> p (j n)").bitcast(FP8X4),
                 scales=b_scales[:].rearrange("p j n -> p (j n)"),
-                in_=grouped["x2"][:].rearrange("p j n t -> p (j n t)"),
+                in_=b_grouped[:].rearrange("p j n t -> p (j n t)"),
             )
 
-        def quantise_x1(i):
-            nc.vector.quantize_mx(
-                out=a_codes[:, i, :].bitcast(FP8X4),
-                scales=a_scales[:, i, :],
-                in_=grouped[X2_TILES + i][:].rearrange("p n t -> p (n t)"),
+        def flip_x1(k):
+            pairs[k] = psum_flip.tile([P, 2, PAIR], F32, name="flipped", tag="flipped")
+            for h in range(2):
+                words = x1_sb[:, 2 * k + h, :].bitcast(F32)
+                for u in range(2):
+                    nc.tensor.transpose(
+                        pairs[k][:, u, h * P : (h + 1) * P], words[:, u * P : (u + 1) * P], ident[:]
+                    )
+
+        def scale_x1(k):
+            a_grouped[k] = work.tile([P, PAIR, 2, 2], BF16, name="a_grouped", tag="a_grouped", align_bytes=64)
+            nc.vector.tensor_tensor(
+                out=a_grouped[k][:],
+                in0=pairs[k][:].rearrange("p u n -> p (u n)").bitcast(BF16).rearrange("p (u n e) -> p n u e", u=2, e=2),
+                in1=inv_l[:].rearrange("p o (u e) -> p o u e", e=2).to_broadcast([P, PAIR, 2, 2]),
+                op=ALU.mult,
             )
+
+        def quantise_x1(k):
+            nc.vector.quantize_mx(
+                out=a_codes[:, 2 * k : 2 * k + 2, :].rearrange("p i n -> p (i n)").bitcast(FP8X4),
+                scales=a_scales[:, 2 * k : 2 * k + 2, :].rearrange("p i n -> p (i n)"),
+                in_=a_grouped[k][:].rearrange("p n u e -> p (n u e)"),
+            )
+
+        def scale_rows_x1(i):
+            scaled["x1", i] = work.tile([P, D], F32, name="scaled_x1", tag="scaled_x1")
+            nc.gpsimd.tensor_tensor(
+                out=scaled["x1", i][:],
+                in0=x1_sb[:, i, :],
+                in1=inv_l_sb[:].rearrange("q u p e -> q (u p e)"),
+                op=ALU.mult,
+            )
+
+        def sum_squares_x1(i):
+            sum_squares(scaled["x1", i][:], sq1[:, i : i + 1])
 
         def multiply(i):
             cross[i] = psum_cross.tile([P, N2], F32, name="cross", tag="cross")
@@ -191,75 +193,107 @@ def tile_matern52_s_kernel(tc, X1, X2, c, l, out):
 
         def clamp(i):
             d2[i] = work.tile([P, N2], F32, name="d2", tag="d2")
-            engine = nc.gpsimd if i in CLAMP_G else nc.vector
-            engine.tensor_scalar(
+            nc.vector.tensor_scalar(
                 out=d2[i][:], in0=part[i][:], scalar1=sq1[:, i : i + 1], scalar2=0.0, op0=ALU.add, op1=ALU.max
             )
 
         def root(i):
-            nc.scalar.activation(out=s_all[:, i, :], in_=d2[i][:], func=ACT.Sqrt, scale=kk_5)
+            nc.scalar.activation(out=sigma_all[:, i, :], in_=d2[i][:], func=ACT.Sqrt, scale=kk_5)
 
-        def polynomial(i):
-            nc.scalar.activation(
-                out=w_all[:, i, :], in_=s_all[:, i, :], func=ACT.Square, bias=k_15
-            )
+        def scalar_polynomial(i):
+            nc.scalar.activation(out=w_all[:, i, :], in_=sigma_all[:, i, :], func=ACT.Square, bias=k_15)
 
         def vector_polynomial(i):
             nc.vector.scalar_tensor_tensor(
                 out=w_all[:, i, :],
-                in0=s_all[:, i, :],
+                in0=sigma_all[:, i, :],
                 scalar=k_30,
-                in1=s_all[:, i, :],
+                in1=sigma_all[:, i, :],
                 op0=ALU.add,
                 op1=ALU.mult,
             )
 
-        def decay_finish_store(i, first, last):
+        def decay_finish_store(i, columns):
             decay = work.tile([P, N2], F32, name="decay", tag="decay")
-            columns = slice(first, last)
-            nc.scalar.activation(out=decay[:, columns], in_=s_all[:, i, columns], func=ACT.Exp, scale=exp_scale[:])
+            nc.scalar.activation(out=decay[:, columns], in_=sigma_all[:, i, columns], func=ACT.Exp, scale=exp_scale[:])
             nc.vector.scalar_tensor_tensor(
                 out=result_all[:, i, columns],
                 in0=w_all[:, i, columns],
-                scalar=kk_075 if i < X1_TILES - VECTOR_POLYNOMIALS else kk_3,
+                scalar=kk_075 if i < SCALAR_POLYNOMIALS else kk_3,
                 in1=decay[:, columns],
                 op0=ALU.add,
                 op1=ALU.mult,
             )
             nc.sync.dma_start(out=out_view[:, i, columns], in_=result_all[:, i, columns])
 
-        def due(stage, index, count):
-            if 0 <= index < count:
-                stage(index)
-
-        for k in range(POINT_TILES + ROOT_LAG + 4):
-            i = k - X2_TILES
-            now = [tile for tile in range(X1_TILES) if min(tile + MULTIPLY_LAG, X1_TILES + QUANTISE_LAG) == i]
-            for tile in now:
-                multiply(tile)
-            if k == X2_TILES + 1:
-                rows_of["sq2"] = repeat_on_all_partitions(sq2, X2_TILES)
-            due(scale, k, POINT_TILES)
-            due(regroup, k - REGROUP_LAG, POINT_TILES)
-            due(flip, k, POINT_TILES)
-            for tile in now:
-                bracket(tile)
-            due(root, i - ROOT_LAG, X1_TILES)
-            if k == QB:
-                quantise_x2()
-            due(quantise_x1, i - QUANTISE_LAG, X1_TILES)
-            due(sum_squares, k, POINT_TILES)
-            for tile in now:
-                clamp(tile)
-            due(polynomial, i - ROOT_LAG - 1, X1_TILES - VECTOR_POLYNOMIALS)
-            if k == X2_TILES + 2:
-                nc.scalar.copy(out=sq2_rows[:], in_=rows_of["sq2"][:])
-
+        for i in range(X1_TILES):
+            scale_rows_x1(i)
+        flip_x1(0)
+        for j in range(X2_TILES):
+            scale_x2(j)
+        flip_x2(0)
+        flip_x2(1)
+        flip_x1(1)
+        for j in (0, 1):
+            sum_squares_x2(j)
+        for j in (0, 1):
+            regroup_x2(j)
+        scale_x1(0)
+        nc.vector.scalar_tensor_tensor(
+            out=c_abs[:], in0=c_sb[:], scalar=-1.0, in1=c_sb[:], op0=ALU.mult, op1=ALU.max
+        )
+        flip_x2(2)
+        flip_x2(3)
+        for j in (2, 3):
+            sum_squares_x2(j)
+        for j in (2, 3):
+            regroup_x2(j)
+        scale_x1(1)
+        nc.vector.tensor_scalar(
+            out=k_sb[:], in0=c_abs[:], scalar1=1e-15, scalar2=1.0 / math.sqrt(3.0), op0=ALU.max, op1=ALU.mult
+        )
+        quantise_x1(0)
+        quantise_x1(1)
+        nc.vector.tensor_scalar(
+            out=kk_all[:], in0=square_factors[:], scalar1=k_sb[:], scalar2=k_sb[:], op0=ALU.mult, op1=ALU.mult
+        )
+        nc.vector.tensor_scalar(
+            out=k_all[:], in0=factors[:], scalar1=k_sb[:], scalar2=0.0, op0=ALU.mult, op1=ALU.add
+        )
+        flip_x1(2)
+        sq2_rows_ps = repeat_on_all_partitions(sq2, X2_TILES)
+        scale_x1(2)
         nc.vector.reciprocal(out=exp_scale[:], in_=k_minus)
-        for i in range(X1_TILES - VECTOR_POLYNOMIALS, X1_TILES):
-            vector_polynomial(i)
+        quantise_x2()
+        flip_x1(3)
+        multiply(0)
+        multiply(1)
+        scale_x1(3)
+        for i in (0, 1):
+            sum_squares_x1(i)
+        nc.scalar.copy(out=sq2_rows[:], in_=sq2_rows_ps[:])
+        for i in (2, 3, 4):
+            sum_squares_x1(i)
 
+        for i in range(X1_TILES + 1):
+            if i < X1_TILES:
+                bracket(i)
+            if i + 2 < X1_TILES:
+                multiply(i + 2)
+            if i < 2:
+                quantise_x1(i + 2)
+            ready = i if i < 2 else i - 1
+            if i != 2:
+                clamp(ready)
+                root(ready)
+                if 1 <= ready <= 3:
+                    sum_squares_x1(ready + 4)
+                if 1 <= ready <= SCALAR_POLYNOMIALS:
+                    scalar_polynomial(ready - 1)
+
+        for i in range(SCALAR_POLYNOMIALS, X1_TILES):
+            vector_polynomial(i)
         for i in range(X1_TILES - 1):
-            decay_finish_store(i, 0, N2)
+            decay_finish_store(i, slice(0, N2))
         for half in range(2):
-            decay_finish_store(X1_TILES - 1, half * N2 // 2, (half + 1) * N2 // 2)
+            decay_finish_store(X1_TILES - 1, slice(half * N2 // 2, (half + 1) * N2 // 2))

@@ -288,8 +288,8 @@ def tile_matern52_s_kernel(tc, X1, X2, c, l, out):
                 root(ready)
                 if 1 <= ready <= 3:
                     sum_squares_x1(ready + 4)
-                if 1 <= ready <= SCALAR_POLYNOMIALS:
-                    scalar_polynomial(ready - 1)
+                if ready < SCALAR_POLYNOMIALS:
+                    scalar_polynomial(ready)
 
         for i in range(SCALAR_POLYNOMIALS, X1_TILES):
             vector_polynomial(i)

@@ -20,6 +20,7 @@ X1_TILES = N1 // P
 X2_TILES = N2 // P
 X1_PAIRS = X1_TILES // 2
 PAIR = 2 * P
+WARM_UP_PRODUCTS = 4
 SCALAR_POLYNOMIALS = 2
 
 FLOPS = 2 * N1 * N2 * D
@@ -38,7 +39,7 @@ def tile_matern52_s_kernel(tc, X1, X2, c, l, out):
         l_sb = keep.tile([P, 2, 2], BF16)
         nc.sync.dma_start(out=l_sb[:], in_=l.rearrange("(u p e) -> p u e", u=2, e=2))
         c_sb = keep.tile([P, 1], BF16)
-        nc.scalar.dma_start(out=c_sb[:], in_=c.partition_broadcast(P))
+        nc.sync.dma_start(out=c_sb[:], in_=c.partition_broadcast(P))
         x2_sb = keep.tile([P, X2_TILES, D], BF16)
         x2_view = X2.rearrange("(j p) d -> p j d", p=P)
         x1_sb = keep.tile([P, X1_TILES, D], BF16)
@@ -54,6 +55,11 @@ def tile_matern52_s_kernel(tc, X1, X2, c, l, out):
         ):
             nc.sync.dma_start(out=x_sb[:, 2 * k : 2 * k + 2, :], in_=view[:, 2 * k : 2 * k + 2, :])
 
+        zeros = keep.tile([P, P], F32)
+        nc.gpsimd.memset(zeros[:], 0.0)
+        unread = psum_cross.tile([P, N2], F32, name="unread", tag="cross")
+        for n in range(WARM_UP_PRODUCTS):
+            nc.tensor.matmul(out=unread[:, :P], lhsT=zeros[:], rhs=zeros[:], start=True, stop=True)
         ident = keep.tile([P, P], F32)
         make_identity(nc, ident[:])
         one = keep.tile([P, 1], F32)
@@ -71,6 +77,19 @@ def tile_matern52_s_kernel(tc, X1, X2, c, l, out):
             for j in range(count):
                 nc.tensor.transpose(rows[:, j, :], columns[:, j : j + 1].to_broadcast([P, P]), ident[:])
             return rows
+
+        k_sb = keep.tile([P, 1], F32)
+        nc.scalar.activation(out=k_sb[:], in_=c_sb[:], func=ACT.Abs, scale=1.0 / math.sqrt(3.0))
+        k_all = keep.tile([P, 3], F32)
+        nc.scalar.activation(out=k_all[:], in_=factors[:], func=ACT.Copy, scale=k_sb[:])
+        kk_half = keep.tile([P, 3], F32)
+        nc.scalar.activation(out=kk_half[:], in_=square_factors[:], func=ACT.Copy, scale=k_sb[:])
+        kk_all = keep.tile([P, 3], F32)
+        nc.scalar.activation(out=kk_all[:], in_=kk_half[:], func=ACT.Copy, scale=k_sb[:])
+        kk_5, kk_3, kk_075 = (kk_all[:, column : column + 1] for column in range(3))
+        k_15, k_30, k_minus = (k_all[:, column : column + 1] for column in range(3))
+        k_below = keep.tile([P, 1], F32)
+        exp_scale = keep.tile([P, 1], F32)
 
         inv_l = keep.tile([P, 1, PACK], F32)
         nc.vector.reciprocal(out=inv_l[:, 0, :], in_=l_sb[:].rearrange("p u e -> p (u e)"))
@@ -90,13 +109,6 @@ def tile_matern52_s_kernel(tc, X1, X2, c, l, out):
         sigma_all = keep.tile([P, X1_TILES, N2], F32)
         w_all = keep.tile([P, X1_TILES, N2], F32)
         result_all = keep.tile([P, X1_TILES, N2], F32)
-        c_abs = keep.tile([P, 1], F32)
-        k_sb = keep.tile([P, 1], F32)
-        kk_all = keep.tile([P, 3], F32)
-        k_all = keep.tile([P, 3], F32)
-        exp_scale = keep.tile([P, 1], F32)
-        kk_5, kk_3, kk_075 = (kk_all[:, column : column + 1] for column in range(3))
-        k_15, k_30, k_minus = (k_all[:, column : column + 1] for column in range(3))
 
         scaled, flipped, pairs, a_grouped, rows_of, cross, part, d2 = {}, {}, {}, {}, {}, {}, {}, {}
 
@@ -239,31 +251,18 @@ def tile_matern52_s_kernel(tc, X1, X2, c, l, out):
         for j in (0, 1):
             regroup_x2(j)
         scale_x1(0)
-        nc.vector.scalar_tensor_tensor(
-            out=c_abs[:], in0=c_sb[:], scalar=-1.0, in1=c_sb[:], op0=ALU.mult, op1=ALU.max
-        )
         flip_x2(2)
+        flip_x1(2)
         flip_x2(3)
         for j in (2, 3):
             sum_squares_x2(j)
         for j in (2, 3):
             regroup_x2(j)
         scale_x1(1)
-        nc.vector.tensor_scalar(
-            out=k_sb[:], in0=c_abs[:], scalar1=1e-15, scalar2=1.0 / math.sqrt(3.0), op0=ALU.max, op1=ALU.mult
-        )
         quantise_x1(0)
         quantise_x1(1)
-        nc.vector.tensor_scalar(
-            out=kk_all[:], in0=square_factors[:], scalar1=k_sb[:], scalar2=k_sb[:], op0=ALU.mult, op1=ALU.mult
-        )
-        nc.vector.tensor_scalar(
-            out=k_all[:], in0=factors[:], scalar1=k_sb[:], scalar2=0.0, op0=ALU.mult, op1=ALU.add
-        )
-        flip_x1(2)
         sq2_rows_ps = repeat_on_all_partitions(sq2, X2_TILES)
         scale_x1(2)
-        nc.vector.reciprocal(out=exp_scale[:], in_=k_minus)
         quantise_x2()
         flip_x1(3)
         multiply(0)
@@ -291,7 +290,12 @@ def tile_matern52_s_kernel(tc, X1, X2, c, l, out):
                 if ready < SCALAR_POLYNOMIALS:
                     scalar_polynomial(ready)
 
-        for i in range(SCALAR_POLYNOMIALS, X1_TILES):
+        nc.vector.tensor_scalar(
+            out=k_below[:], in0=k_minus, scalar1=-1e-15, scalar2=0.0, op0=ALU.min, op1=ALU.add
+        )
+        vector_polynomial(SCALAR_POLYNOMIALS)
+        nc.vector.reciprocal(out=exp_scale[:], in_=k_below[:])
+        for i in range(SCALAR_POLYNOMIALS + 1, X1_TILES):
             vector_polynomial(i)
         for i in range(X1_TILES - 1):
             decay_finish_store(i, slice(0, N2))

import math
from contextlib import ExitStack

import concourse.mybir as mybir
from concourse.masks import make_identity

F32 = mybir.dt.float32
BF16 = mybir.dt.bfloat16
U32 = mybir.dt.uint32
U8 = mybir.dt.uint8
FP8X4 = mybir.dt.float8_e4m3fn_x4
ALU = mybir.AluOpType
ACT = mybir.ActivationFunctionType

P = 128
PACK = 4
N1, N2, D = 1024, 512, 512
assert D == P * PACK
X1_TILES = N1 // P
X2_TILES = N2 // P
X1_PAIRS = X1_TILES // 2
PAIR = 2 * P
WARM_UP_PRODUCTS = 4
SCALAR_POLYNOMIALS = 2

FLOPS = 2 * N1 * N2 * D


def tile_matern52_s_kernel(tc, X1, X2, c, l, out):
    nc = tc.nc
    with ExitStack() as stack:
        keep = stack.enter_context(tc.tile_pool(name="keep", bufs=1))
        work = stack.enter_context(tc.tile_pool(name="work", bufs=4))
        psum_flip = stack.enter_context(tc.psum_pool(name="psum_flip", bufs=4))
        psum_rows = stack.enter_context(tc.psum_pool(name="psum_rows", bufs=2))
        psum_cross = stack.enter_context(tc.psum_pool(name="psum_cross", bufs=2))
        stack.enter_context(tc.manual_schedule())

        l_sb = keep.tile([P, 2, 2], BF16)
        nc.sync.dma_start(out=l_sb[:], in_=l.rearrange("(u p e) -> p u e", u=2, e=2))
        c_sb = keep.tile([P, 1], BF16)
        nc.sync.dma_start(out=c_sb[:], in_=c.partition_broadcast(P))
        x2_sb = keep.tile([P, X2_TILES, D], BF16)
        x2_view = X2.rearrange("(j p) d -> p j d", p=P)
        x1_sb = keep.tile([P, X1_TILES, D], BF16)
        x1_view = X1.rearrange("(p i) d -> p i d", i=X1_TILES)
        out_view = out.rearrange("(p i) m -> p i m", i=X1_TILES)
        for x_sb, view, k in (
            (x2_sb, x2_view, 0),
            (x1_sb, x1_view, 0),
            (x2_sb, x2_view, 1),
            (x1_sb, x1_view, 1),
            (x1_sb, x1_view, 2),
            (x1_sb, x1_view, 3),
        ):
            nc.sync.dma_start(out=x_sb[:, 2 * k : 2 * k + 2, :], in_=view[:, 2 * k : 2 * k + 2, :])

        zeros = keep.tile([P, P], F32)
        nc.gpsimd.memset(zeros[:], 0.0)
        unread = psum_cross.tile([P, N2], F32, name="unread", tag="cross")
        for n in range(WARM_UP_PRODUCTS):
            nc.tensor.matmul(out=unread[:, :P], lhsT=zeros[:], rhs=zeros[:], start=True, stop=True)
        ident = keep.tile([P, P], F32)
        make_identity(nc, ident[:])
        one = keep.tile([P, 1], F32)
        nc.vector.memset(one[:], 1.0)
        warm = keep.tile([P, 1], F32)
        nc.scalar.activation(out=warm[:], in_=one[:], func=ACT.Sqrt)
        square_factors = keep.tile([P, 3], F32)
        factors = keep.tile([P, 3], F32)
        for column, (square_factor, factor) in enumerate(((5.0, 1.5), (3.0, 3.0), (0.75, -1.0))):
            nc.vector.memset(square_factors[:, column : column + 1], square_factor)
            nc.vector.memset(factors[:, column : column + 1], factor)

        def repeat_on_all_partitions(columns, count):
            rows = psum_rows.tile([P, count, P], F32, name="rows", tag="rows")
            for j in range(count):
                nc.tensor.transpose(rows[:, j, :], columns[:, j : j + 1].to_broadcast([P, P]), ident[:])
            return rows

        k_sb = keep.tile([P, 1], F32)
        nc.scalar.activation(out=k_sb[:], in_=c_sb[:], func=ACT.Abs, scale=1.0 / math.sqrt(3.0))
        k_all = keep.tile([P, 3], F32)
        nc.scalar.activation(out=k_all[:], in_=factors[:], func=ACT.Copy, scale=k_sb[:])
        kk_half = keep.tile([P, 3], F32)
        nc.scalar.activation(out=kk_half[:], in_=square_factors[:], func=ACT.Copy, scale=k_sb[:])
        kk_all = keep.tile([P, 3], F32)
        nc.scalar.activation(out=kk_all[:], in_=kk_half[:], func=ACT.Copy, scale=k_sb[:])
        kk_5, kk_3, kk_075 = (kk_all[:, column : column + 1] for column in range(3))
        k_15, k_30, k_minus = (k_all[:, column : column + 1] for column in range(3))
        k_below = keep.tile([P, 1], F32)
        exp_scale = keep.tile([P, 1], F32)

        inv_l = keep.tile([P, 1, PACK], F32)
        nc.vector.reciprocal(out=inv_l[:, 0, :], in_=l_sb[:].rearrange("p u e -> p (u e)"))
        inv_l_rows = repeat_on_all_partitions(inv_l[:, 0, :], PACK)
        inv_l_copy = repeat_on_all_partitions(inv_l[:, 0, :], PACK)
        inv_l_sb = keep.tile([P, 2, P, 2], F32)
        nc.scalar.copy(out=inv_l_sb[:], in_=inv_l_copy[:].rearrange("q (u e) p -> q u p e", u=2))

        a_codes = keep.tile([P, X1_TILES, P], U32, align_bytes=64)
        a_scales = keep.tile([P, X1_TILES, P], U8, align_bytes=64)
        b_codes = keep.tile([P, X2_TILES, P], U32, align_bytes=64)
        b_scales = keep.tile([P, X2_TILES, P], U8, align_bytes=64)
        b_grouped = keep.tile([P, X2_TILES, P, PACK], BF16, align_bytes=64)
        sq1 = keep.tile([P, X1_TILES], F32)
        sq2 = keep.tile([P, X2_TILES], F32)
        sq2_rows = keep.tile([P, X2_TILES, P], F32)
        sigma_all = keep.tile([P, X1_TILES, N2], F32)
        w_all = keep.tile([P, X1_TILES, N2], F32)
        result_all = keep.tile([P, X1_TILES, N2], F32)

        scaled, flipped, pairs, a_grouped, rows_of, cross, part, d2 = {}, {}, {}, {}, {}, {}, {}, {}

        def scale_x2(j):
            scaled["x2", j] = work.tile([P, PACK, P], F32, name="scaled_x2", tag="scaled_x2")
            nc.vector.tensor_tensor(
                out=scaled["x2", j][:].rearrange("n (u e) p -> n u e p", u=2),
                in0=x2_sb[:, j, :].rearrange("n (u p e) -> n u e p", u=2, e=2),
                in1=inv_l_rows[:].rearrange("q (u e) p -> q u e p", u=2),
                op=ALU.mult,
            )

        def flip_x2(j):
            flipped[j] = psum_flip.tile([P, PACK, P], F32, name="flipped", tag="flipped")
            for t in range(PACK):
                nc.tensor.transpose(flipped[j][:, t, :], scaled["x2", j][:, t, :], ident[:])

        def sum_squares(values, column):
            squares = work.tile([P, D], F32, name="squares", tag="squares")
            nc.scalar.activation(out=squares[:], in_=values, func=ACT.Square, accum_out=column)

        def sum_squares_x2(j):
            sum_squares(scaled["x2", j][:].rearrange("n t p -> n (t p)"), sq2[:, j : j + 1])

        def regroup_x2(j):
            nc.scalar.copy(out=b_grouped[:, j, :, :], in_=flipped[j][:].rearrange("p t n -> p n t"))

        def quantise_x2():
            nc.vector.quantize_mx(
                out=b_codes[:].rearrange("p j n -> p (j n)").bitcast(FP8X4),
                scales=b_scales[:].rearrange("p j n -> p (j n)"),
                in_=b_grouped[:].rearrange("p j n t -> p (j n t)"),
            )

        def flip_x1(k):
            pairs[k] = psum_flip.tile([P, 2, PAIR], F32, name="flipped", tag="flipped")
            for h in range(2):
                words = x1_sb[:, 2 * k + h, :].bitcast(F32)
                for u in range(2):
                    nc.tensor.transpose(
                        pairs[k][:, u, h * P : (h + 1) * P], words[:, u * P : (u + 1) * P], ident[:]
                    )

        def scale_x1(k):
            a_grouped[k] = work.tile([P, PAIR, 2, 2], BF16, name="a_grouped", tag="a_grouped", align_bytes=64)
            nc.vector.tensor_tensor(
                out=a_grouped[k][:],
                in0=pairs[k][:].rearrange("p u n -> p (u n)").bitcast(BF16).rearrange("p (u n e) -> p n u e", u=2, e=2),
                in1=inv_l[:].rearrange("p o (u e) -> p o u e", e=2).to_broadcast([P, PAIR, 2, 2]),
                op=ALU.mult,
            )

        def quantise_x1(k):
            nc.vector.quantize_mx(
                out=a_codes[:, 2 * k : 2 * k + 2, :].rearrange("p i n -> p (i n)").bitcast(FP8X4),
                scales=a_scales[:, 2 * k : 2 * k + 2, :].rearrange("p i n -> p (i n)"),
                in_=a_grouped[k][:].rearrange("p n u e -> p (n u e)"),
            )

        def scale_rows_x1(i):
            scaled["x1", i] = work.tile([P, D], F32, name="scaled_x1", tag="scaled_x1")
            nc.gpsimd.tensor_tensor(
                out=scaled["x1", i][:],
                in0=x1_sb[:, i, :],
                in1=inv_l_sb[:].rearrange("q u p e -> q (u p e)"),
                op=ALU.mult,
            )

        def sum_squares_x1(i):
            sum_squares(scaled["x1", i][:], sq1[:, i : i + 1])

        def multiply(i):
            cross[i] = psum_cross.tile([P, N2], F32, name="cross", tag="cross")
            nc.tensor.matmul_mx(
                out=cross[i][:],
                lhsT=a_codes[:, i, :].bitcast(FP8X4),
                lhsT_scale=a_scales[:, i, :],
                rhs=b_codes[:].rearrange("p j n -> p (j n)").bitcast(FP8X4),
                rhs_scale=b_scales[:].rearrange("p j n -> p (j n)"),
                start=True,
                stop=True,
            )

        def bracket(i):
            part[i] = work.tile([P, N2], F32, name="part", tag="part")
            nc.vector.scalar_tensor_tensor(
                out=part[i][:],
                in0=cross[i][:],
                scalar=-2.0,
                in1=sq2_rows[:].rearrange("p j n -> p (j n)"),
                op0=ALU.mult,
                op1=ALU.add,
            )

        def clamp(i):
            d2[i] = work.tile([P, N2], F32, name="d2", tag="d2")
            nc.vector.tensor_scalar(
                out=d2[i][:], in0=part[i][:], scalar1=sq1[:, i : i + 1], scalar2=0.0, op0=ALU.add, op1=ALU.max
            )

        def root(i):
            nc.scalar.activation(out=sigma_all[:, i, :], in_=d2[i][:], func=ACT.Sqrt, scale=kk_5)

        def scalar_polynomial(i):
            nc.scalar.activation(out=w_all[:, i, :], in_=sigma_all[:, i, :], func=ACT.Square, bias=k_15)

        def vector_polynomial(i):
            nc.vector.scalar_tensor_tensor(
                out=w_all[:, i, :],
                in0=sigma_all[:, i, :],
                scalar=k_30,
                in1=sigma_all[:, i, :],
                op0=ALU.add,
                op1=ALU.mult,
            )

        def decay_finish_store(i, columns):
            decay = work.tile([P, N2], F32, name="decay", tag="decay")
            nc.scalar.activation(out=decay[:, columns], in_=sigma_all[:, i, columns], func=ACT.Exp, scale=exp_scale[:])
            nc.vector.scalar_tensor_tensor(
                out=result_all[:, i, columns],
                in0=w_all[:, i, columns],
                scalar=kk_075 if i < SCALAR_POLYNOMIALS else kk_3,
                in1=decay[:, columns],
                op0=ALU.add,
                op1=ALU.mult,
            )
            nc.sync.dma_start(out=out_view[:, i, columns], in_=result_all[:, i, columns])

        for i in range(X1_TILES):
            scale_rows_x1(i)
        flip_x1(0)
        for j in range(X2_TILES):
            scale_x2(j)
        flip_x2(0)
        flip_x2(1)
        flip_x1(1)
        for j in (0, 1):
            sum_squares_x2(j)
        for j in (0, 1):
            regroup_x2(j)
        scale_x1(0)
        flip_x2(2)
        flip_x1(2)
        flip_x2(3)
        for j in (2, 3):
            sum_squares_x2(j)
        for j in (2, 3):
            regroup_x2(j)
        scale_x1(1)
        quantise_x1(0)
        quantise_x1(1)
        sq2_rows_ps = repeat_on_all_partitions(sq2, X2_TILES)
        scale_x1(2)
        quantise_x2()
        flip_x1(3)
        multiply(0)
        multiply(1)
        scale_x1(3)
        for i in (0, 1):
            sum_squares_x1(i)
        nc.scalar.copy(out=sq2_rows[:], in_=sq2_rows_ps[:])
        for i in (2, 3, 4):
            sum_squares_x1(i)

        for i in range(X1_TILES + 1):
            if i < X1_TILES:
                bracket(i)
            if i + 2 < X1_TILES:
                multiply(i + 2)
            if i < 2:
                quantise_x1(i + 2)
            ready = i if i < 2 else i - 1
            if i != 2:
                clamp(ready)
                root(ready)
                if 1 <= ready <= 3:
                    sum_squares_x1(ready + 4)
                if ready < SCALAR_POLYNOMIALS:
                    scalar_polynomial(ready)

        nc.vector.tensor_scalar(
            out=k_below[:], in0=k_minus, scalar1=-1e-15, scalar2=0.0, op0=ALU.min, op1=ALU.add
        )
        vector_polynomial(SCALAR_POLYNOMIALS)
        nc.vector.reciprocal(out=exp_scale[:], in_=k_below[:])
        for i in range(SCALAR_POLYNOMIALS + 1, X1_TILES):
            vector_polynomial(i)
        for i in range(X1_TILES - 1):
            decay_finish_store(i, slice(0, N2))
        for half in range(2):
            decay_finish_store(X1_TILES - 1, slice(half * N2 // 2, (half + 1) * N2 // 2))
